import numpy as np
import ml_dtypes


def mxq(x, axis, fmt="e4m3"):
    dtype, down = {"e4m3": (ml_dtypes.float8_e4m3fn, 7), "e5m2": (ml_dtypes.float8_e5m2, 14)}[fmt]
    v = np.moveaxis(np.asarray(x, np.float32).astype(ml_dtypes.bfloat16).astype(np.float64), axis, -1)
    blocks = v.reshape(v.shape[:-1] + (-1, 32))
    amax = np.abs(blocks).max(-1, keepdims=True)
    byte = np.maximum(np.where(amax > 0, np.frexp(amax)[1] - 1 + 127, 0) - down, 1)
    scale = np.exp2(byte - 127.0)
    codes = (blocks / scale).astype(np.float32).astype(dtype).astype(np.float64)
    return np.moveaxis((codes * scale).reshape(v.shape), -1, axis)


WIDE = False


def mx_kscale(k):
    if not WIDE:
        return np.ones(k)
    levels = np.array([10, -10, 5, -5, 0])
    if k % 512:
        return np.exp2(np.random.permutation(np.resize(levels, k // 32))).repeat(32)
    a = np.empty((k // 512, 16))
    for p in range(k // 512):
        a[p, :8] = np.random.permutation(np.resize(levels, 8))
        for g in range(8):
            far = levels[np.abs(levels - a[p, g]) >= 10]
            a[p, g + 8] = far[np.random.randint(len(far))]
    return np.exp2(a.ravel()).repeat(32)


BF16 = ml_dtypes.bfloat16


def bf(x):
    return np.asarray(x, np.float32).astype(BF16)


def f64(x):
    return np.asarray(x).astype(np.float64)


E2M1 = np.array([0.0, 0.5, 1.0, 1.5, 2.0, 3.0, 4.0, 6.0, -0.0, -0.5, -1.0, -1.5, -2.0, -3.0, -4.0, -6.0])


def pack_weight(w, fmt):
    k, n = w.shape
    w = f64(bf(w)).reshape(k // 32, 32, n)
    amax = np.abs(w).max(1)
    if fmt == "e4m3":
        byte = np.frexp(amax)[1] - 1 + 127 - 7
    else:
        mant, ex = np.frexp(amax / 6.0)
        byte = np.where(mant > 0.5, ex, ex - 1) + 127
    byte = np.clip(np.where(amax > 0, byte, 1), 1, 254)
    scaled = (w * np.exp2(127.0 - byte)[:, None, :]).reshape(k, n).astype(np.float32)
    by_word = np.ascontiguousarray(scaled.reshape(k // 512, 128, 4, n).transpose(0, 1, 3, 2))
    if fmt == "e4m3":
        words = by_word.astype(ml_dtypes.float8_e4m3fn).view(np.uint8)
    else:
        c = by_word.astype(ml_dtypes.float4_e2m1fn).view(np.uint8) & 0xF
        words = c[..., 0::2] | (c[..., 1::2] << 4)
    return np.ascontiguousarray(words), np.ascontiguousarray(byte.astype(np.uint8).reshape(k // 512, 16, n))


def unpack_weight(words, scales, fmt):
    g, p, n, _ = words.shape
    if fmt == "e4m3":
        vals = np.ascontiguousarray(words).view(ml_dtypes.float8_e4m3fn).astype(np.float64)
    else:
        nib = np.empty((g, p, n, 4), np.uint8)
        nib[..., 0::2] = words & 0xF
        nib[..., 1::2] = words >> 4
        vals = E2M1[nib]
    vals = vals * np.repeat(np.exp2(scales.astype(np.float64) - 127.0), 8, axis=1)[..., None]
    return vals.transpose(0, 1, 3, 2).reshape(g * 512, n)


G, S, M, H, E, C = 4, 1024, 512, 512, 16, 64


def setup_inputs():
    t = mx_kscale(H)
    u = mx_kscale(E * C).reshape(E, C)
    h = bf(np.maximum(np.random.standard_normal((E, G, C, H)), 0.0) * 1.4 * t * u[:, None, :, None])
    wo = np.random.standard_normal((E, H, M)) * 10.0 / np.sqrt(H * E * C) / t[None, :, None]
    wo_words, wo_scales = pack_weight(wo.reshape(-1, M), "e4m3")
    combined_weights = bf(np.random.standard_normal((G, S, E, C)) * 0.1 / u)
    return {"h": h,
            "wo_words": wo_words,
            "wo_scales": wo_scales,
            "combined_weights": combined_weights}


def reference(h, wo_words, wo_scales, combined_weights):
    wo = unpack_weight(wo_words, wo_scales, "e4m3").reshape(E, H, M)
    eo = mxq(f64(h).reshape(E, G * C, H), 2, "e4m3") @ wo
    expert_outputs = eo.reshape(E, G, C, M).transpose(1, 0, 2, 3)
    cw = mxq(f64(combined_weights).reshape(G, S, E * C), 2, "e4m3")
    return cw @ mxq(expert_outputs.reshape(G, E * C, M), 1, "e4m3")

@@ -1,0 +1,217 @@
+from contextlib import ExitStack
+
+import concourse.mybir as mybir
+from concourse.masks import make_identity
+
+F32 = mybir.dt.float32
+BF16 = mybir.dt.bfloat16
+I32 = mybir.dt.int32
+U32 = mybir.dt.uint32
+U8 = mybir.dt.uint8
+FP8X4 = mybir.dt.float8_e4m3fn_x4
+
+P = 128
+E, G, C, H, M, S = 16, 4, 64, 512, 512, 1024
+ROWS = G * C
+PAIRS = E // 2
+QUADS = E // 4
+S_TILES = S // P
+STEP_TILES = 4
+STEPS = G * S_TILES // STEP_TILES
+STEPS_PER_GROUP = STEPS // G
+EO_LAG = PAIRS // 2 + 1
+
+FLOPS = 2 * E * ROWS * H * M + 2 * G * S * E * C * M
+
+
+def tile_flaxpositionwisemoelayer_pb_t_e_kernel(tc, h, wo_words, wo_scales, combined_weights, out):
+    nc = tc.nc
+    with ExitStack() as ctx:
+        keep = ctx.enter_context(tc.tile_pool(name="keep", bufs=1))
+        stage = ctx.enter_context(tc.tile_pool(name="stage", bufs=4))
+        results = ctx.enter_context(tc.tile_pool(name="results", bufs=10))
+        banks = ctx.enter_context(tc.psum_pool(name="banks", bufs=8))
+        ctx.enter_context(tc.manual_schedule())
+
+        ident_f32 = keep.tile([P, P], F32, name="ident_f32")
+        wo_planes = keep.tile([P, QUADS, M], U8, name="wo_planes", align_bytes=64)
+        h_sb = [keep.tile([P, 2, 2 * H], BF16, name="h_sb%d" % i) for i in range(PAIRS)]
+        wo_sb = [keep.tile([P, 2, M], U32, name="wo_sb%d" % i, align_bytes=64) for i in range(PAIRS)]
+        cw_sb = [keep.tile([P, STEP_TILES, E * C], BF16, name="cw_sb%d" % v) for v in range(STEPS)]
+        eoT_sb = [keep.tile([P, 4 * 2 * G, 2 * P], BF16, name="eoT_sb%d" % a) for a in range(2)]
+        eo_codes = [keep.tile([P, 2, M], U32, name="eo_codes%d" % g, align_bytes=64) for g in range(G)]
+        eo_scales = [keep.tile([P, 2, M], U8, name="eo_scales%d" % g, align_bytes=64) for g in range(G)]
+
+        nc.vector.memset(wo_planes[:].bitcast(I32), 0)
+        make_identity(nc, ident_f32[:])
+
+        def load_h(i):
+            nc.sync.dma_start(
+                out=h_sb[i][:],
+                in_=h[2 * i : 2 * i + 2].rearrange("x g (c2 r) k -> (g c2) x (r k)", r=2),
+            )
+
+        def load_wo(i):
+            nc.sync.dma_start(
+                out=wo_sb[i][:].bitcast(I32),
+                in_=wo_words[2 * i : 2 * i + 2].rearrange("j p n t -> p j (n t)").bitcast(I32),
+            )
+
+        def load_wo_scales(q):
+            for quadrant in range(4):
+                nc.sync.dma_start(
+                    out=wo_planes[32 * quadrant : 32 * quadrant + 16, q, :].bitcast(I32),
+                    in_=wo_scales[4 * q : 4 * q + 4, 4 * quadrant : 4 * quadrant + 4, :].bitcast(I32),
+                )
+
+        load_h(0)
+        load_h(1)
+        for i in range(PAIRS):
+            if i % 2 == 0:
+                load_wo_scales(i // 2)
+            load_wo(i)
+            if i + 2 < PAIRS:
+                load_h(i + 2)
+        for v in range(STEPS):
+            g, part = divmod(v, STEPS_PER_GROUP)
+            rows = combined_weights[g].rearrange("(p r) e c -> p r (e c)", r=S_TILES)
+            nc.sync.dma_start(out=cw_sb[v][:], in_=rows[:, part * STEP_TILES : (part + 1) * STEP_TILES, :])
+
+        hT = {}
+        cwT = {}
+
+        def transpose_h(i):
+            hT_grp = stage.tile([P, 2 * 4 * ROWS], BF16, tag="grouped", align_bytes=64)
+            hT_codes = stage.tile([P, 2 * ROWS], U32, tag="codes", align_bytes=64)
+            hT_scales = stage.tile([P, 2 * ROWS], U8, tag="scales", align_bytes=64)
+            for x in range(2):
+                words = h_sb[i][:, x, :].bitcast(F32)
+                hT_ps = banks.tile([P, 4, P], F32, tag="bank")
+                for r in range(2):
+                    for w in range(2):
+                        nc.tensor.transpose(
+                            hT_ps[:, 2 * r + w, :],
+                            words[:, r * 256 + w : (r + 1) * 256 : 2],
+                            ident_f32[:],
+                        )
+                nc.vector.tensor_copy(
+                    out=hT_grp[:, x * 4 * ROWS : (x + 1) * 4 * ROWS]
+                    .bitcast(F32)
+                    .rearrange("p (u n rw) -> p u n rw", u=2, rw=4),
+                    in_=hT_ps[:].rearrange("p rw (n u) -> p u n rw", u=2),
+                )
+            nc.vector.quantize_mx(out=hT_codes[:].bitcast(FP8X4), scales=hT_scales[:], in_=hT_grp[:])
+            hT[i] = (hT_codes, hT_scales)
+
+        def project(i):
+            hT_codes, hT_scales = hT[i]
+            for x2 in range(2):
+                q, x = divmod(2 * i + x2, 4)
+                rows = slice(x2 * ROWS, (x2 + 1) * ROWS)
+                for mh in range(2):
+                    eoT_ps = banks.tile([P, 2, ROWS], F32, tag="bank")
+                    for m2 in range(2):
+                        cols = slice((2 * mh + m2) * P, (2 * mh + m2 + 1) * P)
+                        nc.tensor.matmul_mx(
+                            out=eoT_ps[:, m2, :],
+                            lhsT=wo_sb[i][:, x2, cols].bitcast(FP8X4),
+                            lhsT_scale=wo_planes[4 * x : P, q, cols],
+                            rhs=hT_codes[:, rows].bitcast(FP8X4),
+                            rhs_scale=hT_scales[:, rows],
+                            start=True,
+                            stop=True,
+                        )
+                    x8 = (2 * i + x2) % 8
+                    kept = eoT_sb[i // 4][:, 4 * G * mh : 4 * G * (mh + 1), 32 * x8 : 32 * (x8 + 1)]
+                    eoT_in = eoT_ps[:].rearrange("p m2 (ug c) -> p (m2 ug) c", c=32)
+                    if 2 * x2 + mh < 3:
+                        nc.scalar.copy(out=kept, in_=eoT_in)
+                    else:
+                        nc.vector.tensor_copy(out=kept, in_=eoT_in)
+
+        def transpose_eo(g, a):
+            eo_grp = stage.tile([P, M, 4], BF16, tag="grouped", align_bytes=64)
+            for mh in range(2):
+                eo_ps = banks.tile([P, 2, 2 * P], F32, tag="bank")
+                for u in range(2):
+                    for m2 in range(2):
+                        nc.tensor.transpose(
+                            eo_ps[:, u, m2 * P : (m2 + 1) * P],
+                            eoT_sb[a][:, ((2 * mh + m2) * 2 + u) * G + g, :].bitcast(F32),
+                            ident_f32[:],
+                        )
+                grouped = eo_grp[:, mh * 2 * P : (mh + 1) * 2 * P, :].bitcast(F32)
+                nc.scalar.copy(out=grouped, in_=eo_ps[:].rearrange("p u m -> p m u"))
+            nc.vector.quantize_mx(
+                out=eo_codes[g][:, a, :].bitcast(FP8X4),
+                scales=eo_scales[g][:, a, :],
+                in_=eo_grp[:].rearrange("p m t -> p (m t)"),
+            )
+
+        def transpose_cw(v):
+            quantised = []
+            for pair in range(STEP_TILES // 2):
+                cw_grp = stage.tile([P, 2 * E * C], BF16, tag="grouped", align_bytes=64)
+                cw_codes = stage.tile([P, 4 * P], U32, tag="codes", align_bytes=64)
+                cw_scales = stage.tile([P, 4 * P], U8, tag="scales", align_bytes=64)
+                for j in range(2):
+                    words = cw_sb[v][:, 2 * pair + j, :].bitcast(F32)
+                    cwT_ps = banks.tile([P, 4, P], F32, tag="bank")
+                    for window in range(4):
+                        nc.tensor.transpose(
+                            cwT_ps[:, window, :],
+                            words[:, 256 * (window // 2) + window % 2 : 256 * (window // 2 + 1) : 2],
+                            ident_f32[:],
+                        )
+                    grouped = (
+                        cw_grp[:, j * E * C : (j + 1) * E * C].bitcast(F32).rearrange("p (a s u) -> p a s u", a=2, u=2)
+                    )
+                    if 2 * pair + j < STEP_TILES - 1:
+                        nc.vector.tensor_copy(out=grouped, in_=cwT_ps[:].rearrange("p (a u) s -> p a s u", u=2))
+                    else:
+                        nc.scalar.copy(out=grouped, in_=cwT_ps[:].rearrange("p (a u) s -> p a s u", u=2))
+                quantised.append((cw_grp, cw_codes, cw_scales))
+            for cw_grp, cw_codes, cw_scales in quantised:
+                nc.vector.quantize_mx(out=cw_codes[:].bitcast(FP8X4), scales=cw_scales[:], in_=cw_grp[:])
+            cwT[v] = quantised
+
+        def combine(v):
+            g, part = divmod(v, STEPS_PER_GROUP)
+            out_rows = out[g].rearrange("(p r) m -> p r m", r=S_TILES)
+            for tile_no in range(STEP_TILES):
+                pair, j = divmod(tile_no, 2)
+                cw_grp, cw_codes, cw_scales = cwT[v][pair]
+                out_ps = banks.tile([P, M], F32, tag="bank")
+                for a in range(2):
+                    cols = slice((2 * j + a) * P, (2 * j + a + 1) * P)
+                    nc.tensor.matmul_mx(
+                        out=out_ps[:],
+                        lhsT=cw_codes[:, cols].bitcast(FP8X4),
+                        lhsT_scale=cw_scales[:, cols],
+                        rhs=eo_codes[g][:, a, :].bitcast(FP8X4),
+                        rhs_scale=eo_scales[g][:, a, :],
+                        start=(a == 0),
+                        stop=(a == 1),
+                    )
+                out_sb = results.tile([P, M], F32)
+                nc.scalar.copy(out=out_sb[:], in_=out_ps[:])
+                nc.sync.dma_start(out=out_rows[:, part * STEP_TILES + tile_no, :], in_=out_sb[:])
+
+        for i in range(PAIRS):
+            transpose_h(i)
+            if i >= EO_LAG:
+                transpose_eo(i - EO_LAG, 0)
+            if i >= 1:
+                project(i - 1)
+        for g in range(PAIRS - EO_LAG, G):
+            transpose_eo(g, 0)
+        project(PAIRS - 1)
+        transpose_cw(0)
+        transpose_eo(0, 1)
+        for v in range(STEPS):
+            g, part = divmod(v, STEPS_PER_GROUP)
+            if v + 1 < STEPS:
+                transpose_cw(v + 1)
+            if part == 0 and g + 1 < G:
+                transpose_eo(g + 1, 1)
+            combine(v)

@@ -28,6 +28,7 @@ def tile_flaxpositionwisemoelayer_pb_t_e_kernel(tc, h, wo_words, wo_scales, comb
     nc = tc.nc
     with ExitStack() as ctx:
         keep = ctx.enter_context(tc.tile_pool(name="keep", bufs=1))
+        rows = ctx.enter_context(tc.tile_pool(name="rows", bufs=8))
         stage = ctx.enter_context(tc.tile_pool(name="stage", bufs=4))
         results = ctx.enter_context(tc.tile_pool(name="results", bufs=10))
         banks = ctx.enter_context(tc.psum_pool(name="banks", bufs=8))
@@ -35,7 +36,7 @@ def tile_flaxpositionwisemoelayer_pb_t_e_kernel(tc, h, wo_words, wo_scales, comb
 
         ident_f32 = keep.tile([P, P], F32, name="ident_f32")
         wo_planes = keep.tile([P, QUADS, M], U8, name="wo_planes", align_bytes=64)
-        h_sb = [keep.tile([P, 2, 2 * H], BF16, name="h_sb%d" % i) for i in range(PAIRS)]
+        h_sb = [rows.tile([P, 2, 2 * H], BF16, name="h_sb%d" % i, tag="rows") for i in range(PAIRS)]
         wo_sb = [keep.tile([P, 2, M], U32, name="wo_sb%d" % i, align_bytes=64) for i in range(PAIRS)]
         cw_sb = [keep.tile([P, STEP_TILES, E * C], BF16, name="cw_sb%d" % v) for v in range(STEPS)]
         eoT_sb = [keep.tile([P, 4 * 2 * G, 2 * P], BF16, name="eoT_sb%d" % a) for a in range(2)]
@@ -74,11 +75,12 @@ def tile_flaxpositionwisemoelayer_pb_t_e_kernel(tc, h, wo_words, wo_scales, comb
                 load_h(i + 2)
         for v in range(STEPS):
             g, part = divmod(v, STEPS_PER_GROUP)
-            rows = combined_weights[g].rearrange("(p r) e c -> p r (e c)", r=S_TILES)
-            nc.sync.dma_start(out=cw_sb[v][:], in_=rows[:, part * STEP_TILES : (part + 1) * STEP_TILES, :])
+            cw_rows = combined_weights[g].rearrange("(p r) e c -> p r (e c)", r=S_TILES)
+            nc.sync.dma_start(out=cw_sb[v][:], in_=cw_rows[:, part * STEP_TILES : (part + 1) * STEP_TILES, :])
 
         hT = {}
         cwT = {}
+        cw_words = {}
 
         def transpose_h(i):
             hT_grp = stage.tile([P, 2 * 4 * ROWS], BF16, tag="grouped", align_bytes=64)
@@ -148,6 +150,19 @@ def tile_flaxpositionwisemoelayer_pb_t_e_kernel(tc, h, wo_words, wo_scales, comb
                 in_=eo_grp[:].rearrange("p m t -> p (m t)"),
             )
 
+        def reorder_cw(v):
+            ordered = []
+            for pair in range(STEP_TILES // 2):
+                cw_ord = rows.tile([P, 2, E * C], BF16, tag="rows")
+                nc.vector.tensor_copy(
+                    out=cw_ord[:].bitcast(F32).rearrange("p j (a u w) -> p (j a) u w", a=2, u=2),
+                    in_=cw_sb[v][:, 2 * pair : 2 * pair + 2, :]
+                    .bitcast(F32)
+                    .rearrange("p j (a w u) -> p (j a) u w", a=2, u=2),
+                )
+                ordered.append(cw_ord)
+            cw_words[v] = ordered
+
         def transpose_cw(v):
             quantised = []
             for pair in range(STEP_TILES // 2):
@@ -155,22 +170,24 @@ def tile_flaxpositionwisemoelayer_pb_t_e_kernel(tc, h, wo_words, wo_scales, comb
                 cw_codes = stage.tile([P, 4 * P], U32, tag="codes", align_bytes=64)
                 cw_scales = stage.tile([P, 4 * P], U8, tag="scales", align_bytes=64)
                 for j in range(2):
-                    words = cw_sb[v][:, 2 * pair + j, :].bitcast(F32)
+                    words = cw_words[v][pair][:, j, :].bitcast(F32)
                     cwT_ps = banks.tile([P, 4, P], F32, tag="bank")
                     for window in range(4):
                         nc.tensor.transpose(
                             cwT_ps[:, window, :],
-                            words[:, 256 * (window // 2) + window % 2 : 256 * (window // 2 + 1) : 2],
+                            words[:, window * P : (window + 1) * P],
                             ident_f32[:],
                         )
                     grouped = (
                         cw_grp[:, j * E * C : (j + 1) * E * C].bitcast(F32).rearrange("p (a s u) -> p a s u", a=2, u=2)
                     )
-                    if 2 * pair + j < STEP_TILES - 1:
+                    if j == 0:
                         nc.vector.tensor_copy(out=grouped, in_=cwT_ps[:].rearrange("p (a u) s -> p a s u", u=2))
                     else:
                         nc.scalar.copy(out=grouped, in_=cwT_ps[:].rearrange("p (a u) s -> p a s u", u=2))
                 quantised.append((cw_grp, cw_codes, cw_scales))
+            if v + 1 < STEPS:
+                reorder_cw(v + 1)
             for cw_grp, cw_codes, cw_scales in quantised:
                 nc.vector.quantize_mx(out=cw_codes[:].bitcast(FP8X4), scales=cw_scales[:], in_=cw_grp[:])
             cwT[v] = quantised
@@ -205,6 +222,7 @@ def tile_flaxpositionwisemoelayer_pb_t_e_kernel(tc, h, wo_words, wo_scales, comb
                 project(i - 1)
         for g in range(PAIRS - EO_LAG, G):
             transpose_eo(g, 0)
+        reorder_cw(0)
         project(PAIRS - 1)
         transpose_cw(0)
         transpose_eo(0, 1)

@@ -65,7 +65,8 @@ def tile_flaxpositionwisemoelayer_pb_t_e_kernel(tc, h, wo_words, wo_scales, comb
                     in_=wo_scales[4 * q : 4 * q + 4, 4 * quadrant : 4 * quadrant + 4, :].bitcast(I32),
                 )
 
-        load_h(0)
+        for x in range(2):
+            nc.sync.dma_start(out=h_sb[0][:, x, :], in_=h[x].rearrange("g (c2 r) k -> (g c2) (r k)", r=2))
         load_h(1)
         for i in range(PAIRS):
             if i % 2 == 0:
@@ -102,7 +103,13 @@ def tile_flaxpositionwisemoelayer_pb_t_e_kernel(tc, h, wo_words, wo_scales, comb
                     .rearrange("p (u n rw) -> p u n rw", u=2, rw=4),
                     in_=hT_ps[:].rearrange("p rw (n u) -> p u n rw", u=2),
                 )
-            nc.vector.quantize_mx(out=hT_codes[:].bitcast(FP8X4), scales=hT_scales[:], in_=hT_grp[:])
+            for x in range(2):
+                cols = slice(x * ROWS, (x + 1) * ROWS)
+                nc.vector.quantize_mx(
+                    out=hT_codes[:, cols].bitcast(FP8X4),
+                    scales=hT_scales[:, cols],
+                    in_=hT_grp[:, x * 4 * ROWS : (x + 1) * 4 * ROWS],
+                )
             hT[i] = (hT_codes, hT_scales)
 
         def project(i):
@@ -216,13 +223,14 @@ def tile_flaxpositionwisemoelayer_pb_t_e_kernel(tc, h, wo_words, wo_scales, comb
 
         for i in range(PAIRS):
             transpose_h(i)
+            if i == PAIRS - 1:
+                reorder_cw(0)
             if i >= EO_LAG:
                 transpose_eo(i - EO_LAG, 0)
             if i >= 1:
                 project(i - 1)
         for g in range(PAIRS - EO_LAG, G):
             transpose_eo(g, 0)
-        reorder_cw(0)
         project(PAIRS - 1)
         transpose_cw(0)
         transpose_eo(0, 1)

@@ -30,6 +30,7 @@ def tile_flaxpositionwisemoelayer_pb_t_e_kernel(tc, h, wo_words, wo_scales, comb
         keep = ctx.enter_context(tc.tile_pool(name="keep", bufs=1))
         rows = ctx.enter_context(tc.tile_pool(name="rows", bufs=8))
         stage = ctx.enter_context(tc.tile_pool(name="stage", bufs=4))
+        codes = ctx.enter_context(tc.tile_pool(name="codes", bufs=8))
         results = ctx.enter_context(tc.tile_pool(name="results", bufs=10))
         banks = ctx.enter_context(tc.psum_pool(name="banks", bufs=8))
         ctx.enter_context(tc.manual_schedule())
@@ -85,8 +86,8 @@ def tile_flaxpositionwisemoelayer_pb_t_e_kernel(tc, h, wo_words, wo_scales, comb
 
         def transpose_h(i):
             hT_grp = stage.tile([P, 2 * 4 * ROWS], BF16, tag="grouped", align_bytes=64)
-            hT_codes = stage.tile([P, 2 * ROWS], U32, tag="codes", align_bytes=64)
-            hT_scales = stage.tile([P, 2 * ROWS], U8, tag="scales", align_bytes=64)
+            hT_codes = codes.tile([P, 2 * ROWS], U32, tag="codes", align_bytes=64)
+            hT_scales = codes.tile([P, 2 * ROWS], U8, tag="scales", align_bytes=64)
             for x in range(2):
                 words = h_sb[i][:, x, :].bitcast(F32)
                 hT_ps = banks.tile([P, 4, P], F32, tag="bank")
@@ -170,19 +171,26 @@ def tile_flaxpositionwisemoelayer_pb_t_e_kernel(tc, h, wo_words, wo_scales, comb
                 ordered.append(cw_ord)
             cw_words[v] = ordered
 
+        def cw_window(v, pair, j, window):
+            if v < 2:
+                row = cw_sb[v][:, 2 * pair + j, :].bitcast(F32)
+                a, u = divmod(window, 2)
+                return row[:, a * 256 + u : (a + 1) * 256 : 2]
+            row = cw_words[v][pair][:, j, :].bitcast(F32)
+            return row[:, window * P : (window + 1) * P]
+
         def transpose_cw(v):
             quantised = []
             for pair in range(STEP_TILES // 2):
                 cw_grp = stage.tile([P, 2 * E * C], BF16, tag="grouped", align_bytes=64)
-                cw_codes = stage.tile([P, 4 * P], U32, tag="codes", align_bytes=64)
-                cw_scales = stage.tile([P, 4 * P], U8, tag="scales", align_bytes=64)
+                cw_codes = codes.tile([P, 4 * P], U32, tag="codes", align_bytes=64)
+                cw_scales = codes.tile([P, 4 * P], U8, tag="scales", align_bytes=64)
                 for j in range(2):
-                    words = cw_words[v][pair][:, j, :].bitcast(F32)
                     cwT_ps = banks.tile([P, 4, P], F32, tag="bank")
                     for window in range(4):
                         nc.tensor.transpose(
                             cwT_ps[:, window, :],
-                            words[:, window * P : (window + 1) * P],
+                            cw_window(v, pair, j, window),
                             ident_f32[:],
                         )
                     grouped = (
@@ -193,8 +201,6 @@ def tile_flaxpositionwisemoelayer_pb_t_e_kernel(tc, h, wo_words, wo_scales, comb
                     else:
                         nc.scalar.copy(out=grouped, in_=cwT_ps[:].rearrange("p (a u) s -> p a s u", u=2))
                 quantised.append((cw_grp, cw_codes, cw_scales))
-            if v + 1 < STEPS:
-                reorder_cw(v + 1)
             for cw_grp, cw_codes, cw_scales in quantised:
                 nc.vector.quantize_mx(out=cw_codes[:].bitcast(FP8X4), scales=cw_scales[:], in_=cw_grp[:])
             cwT[v] = quantised
@@ -223,8 +229,6 @@ def tile_flaxpositionwisemoelayer_pb_t_e_kernel(tc, h, wo_words, wo_scales, comb
 
         for i in range(PAIRS):
             transpose_h(i)
-            if i == PAIRS - 1:
-                reorder_cw(0)
             if i >= EO_LAG:
                 transpose_eo(i - EO_LAG, 0)
             if i >= 1:
@@ -234,10 +238,16 @@ def tile_flaxpositionwisemoelayer_pb_t_e_kernel(tc, h, wo_words, wo_scales, comb
         project(PAIRS - 1)
         transpose_cw(0)
         transpose_eo(0, 1)
-        for v in range(STEPS):
-            g, part = divmod(v, STEPS_PER_GROUP)
-            if v + 1 < STEPS:
-                transpose_cw(v + 1)
-            if part == 0 and g + 1 < G:
-                transpose_eo(g + 1, 1)
+        transpose_cw(1)
+        reorder_cw(2)
+        reorder_cw(3)
+        combine(0)
+        for v in range(2, STEPS, 2):
+            transpose_eo(v // 2, 1)
+            transpose_cw(v)
+            transpose_cw(v + 1)
+            for later in range(v + 2, min(v + 4, STEPS)):
+                reorder_cw(later)
+            combine(v - 1)
             combine(v)
+        combine(STEPS - 1)

@@ -151,7 +151,10 @@ def tile_flaxpositionwisemoelayer_pb_t_e_kernel(tc, h, wo_words, wo_scales, comb
                             ident_f32[:],
                         )
                 grouped = eo_grp[:, mh * 2 * P : (mh + 1) * 2 * P, :].bitcast(F32)
-                nc.scalar.copy(out=grouped, in_=eo_ps[:].rearrange("p u m -> p m u"))
+                if (g, a) == (3, 0):
+                    nc.vector.tensor_copy(out=grouped, in_=eo_ps[:].rearrange("p u m -> p m u"))
+                else:
+                    nc.scalar.copy(out=grouped, in_=eo_ps[:].rearrange("p u m -> p m u"))
             nc.vector.quantize_mx(
                 out=eo_codes[g][:, a, :].bitcast(FP8X4),
                 scales=eo_scales[g][:, a, :],
@@ -233,9 +236,9 @@ def tile_flaxpositionwisemoelayer_pb_t_e_kernel(tc, h, wo_words, wo_scales, comb
                 transpose_eo(i - EO_LAG, 0)
             if i >= 1:
                 project(i - 1)
+        project(PAIRS - 1)
         for g in range(PAIRS - EO_LAG, G):
             transpose_eo(g, 0)
-        project(PAIRS - 1)
         transpose_cw(0)
         transpose_eo(0, 1)
         transpose_cw(1)

from contextlib import ExitStack

import concourse.mybir as mybir
from concourse.masks import make_identity

F32 = mybir.dt.float32
BF16 = mybir.dt.bfloat16
I32 = mybir.dt.int32
U32 = mybir.dt.uint32
U8 = mybir.dt.uint8
FP8X4 = mybir.dt.float8_e4m3fn_x4

P = 128
E, G, C, H, M, S = 16, 4, 64, 512, 512, 1024
ROWS = G * C
PAIRS = E // 2
QUADS = E // 4
S_TILES = S // P
STEP_TILES = 4
STEPS = G * S_TILES // STEP_TILES
STEPS_PER_GROUP = STEPS // G
EO_LAG = PAIRS // 2 + 1

FLOPS = 2 * E * ROWS * H * M + 2 * G * S * E * C * M


def tile_flaxpositionwisemoelayer_pb_t_e_kernel(tc, h, wo_words, wo_scales, combined_weights, out):
    nc = tc.nc
    with ExitStack() as ctx:
        keep = ctx.enter_context(tc.tile_pool(name="keep", bufs=1))
        rows = ctx.enter_context(tc.tile_pool(name="rows", bufs=8))
        stage = ctx.enter_context(tc.tile_pool(name="stage", bufs=4))
        codes = ctx.enter_context(tc.tile_pool(name="codes", bufs=8))
        results = ctx.enter_context(tc.tile_pool(name="results", bufs=10))
        banks = ctx.enter_context(tc.psum_pool(name="banks", bufs=8))
        ctx.enter_context(tc.manual_schedule())

        ident_f32 = keep.tile([P, P], F32, name="ident_f32")
        wo_planes = keep.tile([P, QUADS, M], U8, name="wo_planes", align_bytes=64)
        h_sb = [rows.tile([P, 2, 2 * H], BF16, name="h_sb%d" % i, tag="rows") for i in range(PAIRS)]
        wo_sb = [keep.tile([P, 2, M], U32, name="wo_sb%d" % i, align_bytes=64) for i in range(PAIRS)]
        cw_sb = [keep.tile([P, STEP_TILES, E * C], BF16, name="cw_sb%d" % v) for v in range(STEPS)]
        eoT_sb = [keep.tile([P, 4 * 2 * G, 2 * P], BF16, name="eoT_sb%d" % a) for a in range(2)]
        eo_codes = [keep.tile([P, 2, M], U32, name="eo_codes%d" % g, align_bytes=64) for g in range(G)]
        eo_scales = [keep.tile([P, 2, M], U8, name="eo_scales%d" % g, align_bytes=64) for g in range(G)]

        nc.vector.memset(wo_planes[:].bitcast(I32), 0)
        make_identity(nc, ident_f32[:])

        def load_h(i):
            nc.sync.dma_start(
                out=h_sb[i][:],
                in_=h[2 * i : 2 * i + 2].rearrange("x g (c2 r) k -> (g c2) x (r k)", r=2),
            )

        def load_wo(i):
            nc.sync.dma_start(
                out=wo_sb[i][:].bitcast(I32),
                in_=wo_words[2 * i : 2 * i + 2].rearrange("j p n t -> p j (n t)").bitcast(I32),
            )

        def load_wo_scales(q):
            for quadrant in range(4):
                nc.sync.dma_start(
                    out=wo_planes[32 * quadrant : 32 * quadrant + 16, q, :].bitcast(I32),
                    in_=wo_scales[4 * q : 4 * q + 4, 4 * quadrant : 4 * quadrant + 4, :].bitcast(I32),
                )

        for x in range(2):
            nc.sync.dma_start(out=h_sb[0][:, x, :], in_=h[x].rearrange("g (c2 r) k -> (g c2) (r k)", r=2))
        load_h(1)
        for i in range(PAIRS):
            if i % 2 == 0:
                load_wo_scales(i // 2)
            load_wo(i)
            if i + 2 < PAIRS:
                load_h(i + 2)
        for v in range(STEPS):
            g, part = divmod(v, STEPS_PER_GROUP)
            cw_rows = combined_weights[g].rearrange("(p r) e c -> p r (e c)", r=S_TILES)
            nc.sync.dma_start(out=cw_sb[v][:], in_=cw_rows[:, part * STEP_TILES : (part + 1) * STEP_TILES, :])

        hT = {}
        cwT = {}
        cw_words = {}

        def transpose_h(i):
            hT_grp = stage.tile([P, 2 * 4 * ROWS], BF16, tag="grouped", align_bytes=64)
            hT_codes = codes.tile([P, 2 * ROWS], U32, tag="codes", align_bytes=64)
            hT_scales = codes.tile([P, 2 * ROWS], U8, tag="scales", align_bytes=64)
            for x in range(2):
                words = h_sb[i][:, x, :].bitcast(F32)
                hT_ps = banks.tile([P, 4, P], F32, tag="bank")
                for r in range(2):
                    for w in range(2):
                        nc.tensor.transpose(
                            hT_ps[:, 2 * r + w, :],
                            words[:, r * 256 + w : (r + 1) * 256 : 2],
                            ident_f32[:],
                        )
                nc.vector.tensor_copy(
                    out=hT_grp[:, x * 4 * ROWS : (x + 1) * 4 * ROWS]
                    .bitcast(F32)
                    .rearrange("p (u n rw) -> p u n rw", u=2, rw=4),
                    in_=hT_ps[:].rearrange("p rw (n u) -> p u n rw", u=2),
                )
            for x in range(2):
                cols = slice(x * ROWS, (x + 1) * ROWS)
                nc.vector.quantize_mx(
                    out=hT_codes[:, cols].bitcast(FP8X4),
                    scales=hT_scales[:, cols],
                    in_=hT_grp[:, x * 4 * ROWS : (x + 1) * 4 * ROWS],
                )
            hT[i] = (hT_codes, hT_scales)

        def project(i):
            hT_codes, hT_scales = hT[i]
            for x2 in range(2):
                q, x = divmod(2 * i + x2, 4)
                rows = slice(x2 * ROWS, (x2 + 1) * ROWS)
                for mh in range(2):
                    eoT_ps = banks.tile([P, 2, ROWS], F32, tag="bank")
                    for m2 in range(2):
                        cols = slice((2 * mh + m2) * P, (2 * mh + m2 + 1) * P)
                        nc.tensor.matmul_mx(
                            out=eoT_ps[:, m2, :],
                            lhsT=wo_sb[i][:, x2, cols].bitcast(FP8X4),
                            lhsT_scale=wo_planes[4 * x : P, q, cols],
                            rhs=hT_codes[:, rows].bitcast(FP8X4),
                            rhs_scale=hT_scales[:, rows],
                            start=True,
                            stop=True,
                        )
                    x8 = (2 * i + x2) % 8
                    kept = eoT_sb[i // 4][:, 4 * G * mh : 4 * G * (mh + 1), 32 * x8 : 32 * (x8 + 1)]
                    eoT_in = eoT_ps[:].rearrange("p m2 (ug c) -> p (m2 ug) c", c=32)
                    if 2 * x2 + mh < 3:
                        nc.scalar.copy(out=kept, in_=eoT_in)
                    else:
                        nc.vector.tensor_copy(out=kept, in_=eoT_in)

        def transpose_eo(g, a):
            eo_grp = stage.tile([P, M, 4], BF16, tag="grouped", align_bytes=64)
            for mh in range(2):
                eo_ps = banks.tile([P, 2, 2 * P], F32, tag="bank")
                for u in range(2):
                    for m2 in range(2):
                        nc.tensor.transpose(
                            eo_ps[:, u, m2 * P : (m2 + 1) * P],
                            eoT_sb[a][:, ((2 * mh + m2) * 2 + u) * G + g, :].bitcast(F32),
                            ident_f32[:],
                        )
                grouped = eo_grp[:, mh * 2 * P : (mh + 1) * 2 * P, :].bitcast(F32)
                if (g, a) == (3, 0):
                    nc.vector.tensor_copy(out=grouped, in_=eo_ps[:].rearrange("p u m -> p m u"))
                else:
                    nc.scalar.copy(out=grouped, in_=eo_ps[:].rearrange("p u m -> p m u"))
            nc.vector.quantize_mx(
                out=eo_codes[g][:, a, :].bitcast(FP8X4),
                scales=eo_scales[g][:, a, :],
                in_=eo_grp[:].rearrange("p m t -> p (m t)"),
            )

        def reorder_cw(v):
            ordered = []
            for pair in range(STEP_TILES // 2):
                cw_ord = rows.tile([P, 2, E * C], BF16, tag="rows")
                nc.vector.tensor_copy(
                    out=cw_ord[:].bitcast(F32).rearrange("p j (a u w) -> p (j a) u w", a=2, u=2),
                    in_=cw_sb[v][:, 2 * pair : 2 * pair + 2, :]
                    .bitcast(F32)
                    .rearrange("p j (a w u) -> p (j a) u w", a=2, u=2),
                )
                ordered.append(cw_ord)
            cw_words[v] = ordered

        def cw_window(v, pair, j, window):
            if v < 2:
                row = cw_sb[v][:, 2 * pair + j, :].bitcast(F32)
                a, u = divmod(window, 2)
                return row[:, a * 256 + u : (a + 1) * 256 : 2]
            row = cw_words[v][pair][:, j, :].bitcast(F32)
            return row[:, window * P : (window + 1) * P]

        def transpose_cw(v):
            quantised = []
            for pair in range(STEP_TILES // 2):
                cw_grp = stage.tile([P, 2 * E * C], BF16, tag="grouped", align_bytes=64)
                cw_codes = codes.tile([P, 4 * P], U32, tag="codes", align_bytes=64)
                cw_scales = codes.tile([P, 4 * P], U8, tag="scales", align_bytes=64)
                for j in range(2):
                    cwT_ps = banks.tile([P, 4, P], F32, tag="bank")
                    for window in range(4):
                        nc.tensor.transpose(
                            cwT_ps[:, window, :],
                            cw_window(v, pair, j, window),
                            ident_f32[:],
                        )
                    grouped = (
                        cw_grp[:, j * E * C : (j + 1) * E * C].bitcast(F32).rearrange("p (a s u) -> p a s u", a=2, u=2)
                    )
                    if j == 0:
                        nc.vector.tensor_copy(out=grouped, in_=cwT_ps[:].rearrange("p (a u) s -> p a s u", u=2))
                    else:
                        nc.scalar.copy(out=grouped, in_=cwT_ps[:].rearrange("p (a u) s -> p a s u", u=2))
                quantised.append((cw_grp, cw_codes, cw_scales))
            for cw_grp, cw_codes, cw_scales in quantised:
                nc.vector.quantize_mx(out=cw_codes[:].bitcast(FP8X4), scales=cw_scales[:], in_=cw_grp[:])
            cwT[v] = quantised

        def combine(v):
            g, part = divmod(v, STEPS_PER_GROUP)
            out_rows = out[g].rearrange("(p r) m -> p r m", r=S_TILES)
            for tile_no in range(STEP_TILES):
                pair, j = divmod(tile_no, 2)
                cw_grp, cw_codes, cw_scales = cwT[v][pair]
                out_ps = banks.tile([P, M], F32, tag="bank")
                for a in range(2):
                    cols = slice((2 * j + a) * P, (2 * j + a + 1) * P)
                    nc.tensor.matmul_mx(
                        out=out_ps[:],
                        lhsT=cw_codes[:, cols].bitcast(FP8X4),
                        lhsT_scale=cw_scales[:, cols],
                        rhs=eo_codes[g][:, a, :].bitcast(FP8X4),
                        rhs_scale=eo_scales[g][:, a, :],
                        start=(a == 0),
                        stop=(a == 1),
                    )
                out_sb = results.tile([P, M], F32)
                nc.scalar.copy(out=out_sb[:], in_=out_ps[:])
                nc.sync.dma_start(out=out_rows[:, part * STEP_TILES + tile_no, :], in_=out_sb[:])

        for i in range(PAIRS):
            transpose_h(i)
            if i >= EO_LAG:
                transpose_eo(i - EO_LAG, 0)
            if i >= 1:
                project(i - 1)
        project(PAIRS - 1)
        for g in range(PAIRS - EO_LAG, G):
            transpose_eo(g, 0)
        transpose_cw(0)
        transpose_eo(0, 1)
        transpose_cw(1)
        reorder_cw(2)
        reorder_cw(3)
        combine(0)
        for v in range(2, STEPS, 2):
            transpose_eo(v // 2, 1)
            transpose_cw(v)
            transpose_cw(v + 1)
            for later in range(v + 2, min(v + 4, STEPS)):
                reorder_cw(later)
            combine(v - 1)
            combine(v)
        combine(STEPS - 1)
